import numpy as np
import ml_dtypes

BF16 = ml_dtypes.bfloat16


def bf(x):
    return np.asarray(x, np.float32).astype(BF16)


def f32(x):
    return np.asarray(x, np.float32)


def f64(x):
    return np.asarray(x).astype(np.float64)


def striped(idx):
    return np.tile(idx.reshape(-1, 16).T, (8, 1))


E, L, H, HKV, GQ, D, C, SC, NB, KC, S, RUN, N = 2048, 256, 16, 4, 4, 128, 512, 64, 4, 4, 512, 256, 1024
EPS = 1e-6
SM_N = 1.0


def setup_inputs():
    hidden = f32(np.random.standard_normal((E, L)))
    pre_norm_w = f32(1.0 + 0.1 * np.random.standard_normal((E, 1)))
    wq = bf(np.random.standard_normal((E, E)) / np.sqrt(E))
    wo = bf(3.0 * np.random.standard_normal((E, E)) / np.sqrt(E))
    k_sel = bf(np.random.standard_normal((C, N)))
    v = f32(np.random.standard_normal((C, S)))
    wt = f32(np.repeat(np.repeat(np.random.random((HKV, NB * KC)), D, axis=0), SC, axis=1))
    idx = np.concatenate([np.random.permutation(S)[:RUN] for _ in range(N // RUN)])
    return {'hidden': hidden, 'pre_norm_w': pre_norm_w, 'wq': wq, 'wo': wo, 'k_sel': k_sel, 'v': v, 'wt': wt, 'offs': striped(idx)}


def reference(hidden, pre_norm_w, wq, wo, k_sel, v, wt, offs):
    idx = offs[:16].T.reshape(-1)
    hid = f64(hidden)
    vw = f64(v)[:, idx] * f64(wt)
    xn = hid * f64(pre_norm_w) / np.sqrt(np.mean(hid * hid, axis=0, keepdims=True) + EPS)
    q = f64(wq).T @ xn
    q5 = q.reshape(HKV, GQ, D, NB, SC)
    k5 = f64(k_sel).reshape(HKV, D, NB, KC, SC)
    v5 = vw.reshape(HKV, D, NB, KC, SC)
    s = np.einsum('hadbt,hdbku->habtku', q5, k5) / np.sqrt(D)
    e = np.exp(s)
    p = e / (e.sum(axis=-1, keepdims=True) + SM_N)
    ctx = np.einsum('habtku,hdbku->hadbt', p, v5).reshape(E, L)
    return hid + f64(wo).T @ ctx

@@ -1,0 +1,207 @@
+import math
+from contextlib import ExitStack
+
+import concourse.mybir as mybir
+from concourse.masks import make_identity
+
+F32 = mybir.dt.float32
+BF16 = mybir.dt.bfloat16
+U16 = mybir.dt.uint16
+ALU = mybir.AluOpType
+FN = mybir.ActivationFunctionType
+AXIS_X = mybir.AxisListType.X
+
+P = 128
+E = 2048
+ET = E // P
+L = 256
+HKV = 4
+BLK = 64
+NB = 4
+RUN = 256
+S = 512
+N = 1024
+PIECE = 512
+GRP = 512
+EPS = 1e-6
+SCALE = 1.0 / math.sqrt(P)
+
+FLOPS = 2 * (2 * E * E * L) + 2 * (2 * ET * L * RUN * P)
+
+
+def tile_hierarchicalsparseattention_b_kernel(tc, hidden, pre_norm_w, wq, wo, k_sel, v, wt, offs, out):
+    nc = tc.nc
+    with ExitStack() as ctx:
+        held = ctx.enter_context(tc.tile_pool(name="held", bufs=1))
+        norm_ring = ctx.enter_context(tc.tile_pool(name="norm_ring", bufs=2))
+        work = ctx.enter_context(tc.tile_pool(name="work", bufs=3))
+        acc_psum = ctx.enter_context(tc.psum_pool(name="acc_psum", bufs=4))
+        s_psum = ctx.enter_context(tc.psum_pool(name="s_psum", bufs=2))
+        tp_psum = ctx.enter_context(tc.psum_pool(name="tp_psum", bufs=1))
+        ctx_psum = ctx.enter_context(tc.psum_pool(name="ctx_psum", bufs=1))
+
+        offsets = held.tile([P, N // 16], U16, name="offsets")
+        nc.sync.dma_start(offsets[:], offs)
+
+        w_rows = held.tile([P, P], F32, name="w_rows")
+        nc.vector.memset(w_rows[:], 0.0)
+        nc.sync.dma_start(w_rows[0:ET, :], pre_norm_w.rearrange("(k p) one -> k (p one)", p=P))
+
+        hidden_v = hidden.rearrange("(k p) t -> p k t", p=P)
+        hid = [held.tile([P, 2, L], F32, name=f"hid{c}") for c in range(ET // 2)]
+        for c in range(ET // 2):
+            nc.sync.dma_start(hid[c][:], hidden_v[:, 2 * c : 2 * c + 2, :])
+
+        wq_v = wq.rearrange("(k p) o -> p k o", p=P)
+        wo_v = wo.rearrange("(k p) o -> p k o", p=P)
+        wq_sb = [held.tile([P, ET, GRP], BF16, name=f"wq{g}") for g in range(HKV)]
+        wo_sb = [held.tile([P, ET, GRP], BF16, name=f"wo{g}") for g in range(HKV)]
+        k_sb = [held.tile([P, N], BF16, name=f"k{h}") for h in range(HKV)]
+        v_sb = [held.tile([P, S], F32, name=f"v{h}") for h in range(HKV)]
+        wt_sb = [held.tile([P, N], F32, name=f"wt{h}") for h in range(HKV)]
+
+        def load_weights(tile, view, g):
+            for half in range(2):
+                rows = slice(half * ET // 2, (half + 1) * ET // 2)
+                nc.sync.dma_start(tile[:, rows, :], view[:, rows, g * GRP : (g + 1) * GRP])
+
+        for h in range(HKV):
+            load_weights(wq_sb[h], wq_v, h)
+            nc.sync.dma_start(k_sb[h][:], k_sel[h * P : (h + 1) * P, :])
+            nc.sync.dma_start(v_sb[h][:], v[h * P : (h + 1) * P, :])
+            nc.sync.dma_start(wt_sb[h][:], wt[h * P : (h + 1) * P, :])
+        for g in range(HKV):
+            load_weights(wo_sb[g], wo_v, g)
+
+        ident_f = held.tile([P, P], F32, name="ident_f")
+        make_identity(nc, ident_f[:])
+        ident_b = held.tile([P, P], BF16, name="ident_b")
+        make_identity(nc, ident_b[:])
+        ones_f = held.tile([P, P], F32, name="ones_f")
+        nc.vector.memset(ones_f[:], 1.0)
+        eps_col = held.tile([P, 1], F32, name="eps_col")
+        nc.vector.memset(eps_col[:], EPS)
+
+        ss_ps = acc_psum.tile([P, L], F32, name="ss_ps", tag="acc")
+        for c in range(ET // 2):
+            sq = norm_ring.tile([P, 2, L], F32, name="sq")
+            nc.scalar.activation(sq[:], hid[c][:], FN.Square)
+            sq_sum = norm_ring.tile([P, L], F32, name="sq_sum")
+            nc.vector.tensor_tensor(sq_sum[:], sq[:, 0, :], sq[:, 1, :], ALU.add)
+            nc.tensor.matmul(ss_ps[:], lhsT=ones_f[:], rhs=sq_sum[:], start=(c == 0), stop=(c == ET // 2 - 1))
+        rstd = held.tile([P, L], F32, name="rstd")
+        nc.scalar.activation(rstd[:], ss_ps[:], FN.Abs_reciprocal_sqrt, bias=eps_col[:], scale=1.0 / E)
+
+        w_ps = tp_psum.tile([P, P], F32, name="w_ps", tag="tp")
+        nc.tensor.transpose(w_ps[:], w_rows[:], ident_f[:])
+        w_col = held.tile([P, ET], F32, name="w_col")
+        nc.vector.tensor_copy(w_col[:], w_ps[:, 0:ET])
+
+        xn = [held.tile([P, L], BF16, name=f"xn{e}") for e in range(ET)]
+        for e in range(ET):
+            nc.vector.scalar_tensor_tensor(
+                xn[e][:], hid[e // 2][:, e % 2, :], w_col[:, e : e + 1], rstd[:], op0=ALU.mult, op1=ALU.mult
+            )
+
+        vw_t = [held.tile([P, N // P, P], BF16, name=f"vw_t{h}") for h in range(HKV)]
+        q_sb = [[held.tile([P, NB, 2, BLK], BF16, name=f"q{h}_{u}") for u in range(2)] for h in range(HKV)]
+        ctx_sb = [[held.tile([P, 2, L], BF16, name=f"ctx{h}_{u}") for u in range(2)] for h in range(HKV)]
+
+        def weighted_values(h):
+            for piece in range(N // PIECE):
+                vw = work.tile([P, PIECE], F32, name="vw")
+                nc.vector.tensor_tensor(
+                    vw[:],
+                    v_sb[h][:].indirect(offsets[:, piece * PIECE // 16 : (piece + 1) * PIECE // 16]),
+                    wt_sb[h][:, piece * PIECE : (piece + 1) * PIECE],
+                    ALU.mult,
+                )
+                vw_ps = tp_psum.tile([P, PIECE // P, P], F32, name="vw_ps", tag="tp")
+                for jt in range(PIECE // P):
+                    nc.tensor.transpose(vw_ps[:, jt, :], vw[:, jt * P : (jt + 1) * P], ident_f[:])
+                first = piece * PIECE // P
+                nc.scalar.copy(vw_t[h][:, first : first + PIECE // P, :], vw_ps[:])
+
+        def project_queries(h, u):
+            q_ps = [acc_psum.tile([P, L], F32, name=f"q_ps{a}", tag="acc") for a in range(2)]
+            for e in range(ET):
+                for a in range(2):
+                    col = (2 * u + a) * P
+                    nc.tensor.matmul(
+                        q_ps[a][:], lhsT=wq_sb[h][:, e, col : col + P], rhs=xn[e][:], start=(e == 0), stop=(e == ET - 1)
+                    )
+            for a in range(2):
+                nc.scalar.copy(q_sb[h][u][:, :, a, :], q_ps[a][:].rearrange("p (b t) -> p b t", b=NB))
+
+        def attend(h, u, bp):
+            s_ps = s_psum.tile([P, 2, RUN], F32, name="s_ps")
+            for i in range(2):
+                b = 2 * bp + i
+                nc.tensor.matmul(
+                    s_ps[:, i, :],
+                    lhsT=q_sb[h][u][:, b, :, :].rearrange("p a t -> p (a t)"),
+                    rhs=k_sb[h][:, b * RUN : (b + 1) * RUN],
+                    start=True,
+                    stop=True,
+                )
+            chunks = s_ps[:].rearrange("p i (k c) -> p (i k) c", c=BLK)
+            n_chunks = 2 * RUN // BLK
+            top = work.tile([P, n_chunks], F32, name="top")
+            nc.vector.reduce_max(top[:], chunks, axis=AXIS_X)
+            neg_m = work.tile([P, n_chunks], F32, name="neg_m")
+            nc.vector.tensor_scalar(neg_m[:], top[:], -SCALE, 0.0, op0=ALU.mult, op1=ALU.min)
+            ex = work.tile([P, n_chunks, BLK], F32, name="ex")
+            ex_sum = work.tile([P, n_chunks], F32, name="ex_sum")
+            for c in range(n_chunks):
+                nc.scalar.activation(
+                    ex[:, c, :], chunks[:, c, :], FN.Exp, bias=neg_m[:, c : c + 1], scale=SCALE,
+                    accum_out=ex_sum[:, c : c + 1],
+                )
+            one_term = work.tile([P, n_chunks], F32, name="one_term")
+            nc.scalar.activation(one_term[:], neg_m[:], FN.Exp)
+            den = work.tile([P, n_chunks], F32, name="den")
+            nc.vector.tensor_tensor(den[:], ex_sum[:], one_term[:], ALU.add)
+            rden = work.tile([P, n_chunks], F32, name="rden")
+            nc.vector.reciprocal(rden[:], den[:])
+            prob = work.tile([P, n_chunks, BLK], BF16, name="prob")
+            nc.vector.tensor_tensor(
+                prob[:], ex[:], rden[:].unsqueeze(2).to_broadcast([P, n_chunks, BLK]), ALU.mult
+            )
+            prob_cols = prob[:].rearrange("p k c -> p (k c)")
+            pt_ps = tp_psum.tile([P, 4, P], BF16, name="pt_ps", tag="tp")
+            for jt in range(4):
+                nc.tensor.transpose(pt_ps[:, jt, :], prob_cols[:, jt * P : (jt + 1) * P], ident_b[:])
+            prob_t = work.tile([P, 4, P], BF16, name="prob_t")
+            nc.scalar.copy(prob_t[:], pt_ps[:])
+            c_ps = ctx_psum.tile([P, 2, 2 * BLK], F32, name="c_ps")
+            for i in range(2):
+                b = 2 * bp + i
+                for jt in range(2):
+                    nc.tensor.matmul(
+                        c_ps[:, i, :], lhsT=vw_t[h][:, 2 * b + jt, :], rhs=prob_t[:, 2 * i + jt, :],
+                        start=(jt == 0), stop=(jt == 1),
+                    )
+            nc.vector.tensor_copy(
+                ctx_sb[h][u][:, :, bp * 2 * BLK : (bp + 1) * 2 * BLK].rearrange("p a (i t) -> p a i t", i=2),
+                c_ps[:].rearrange("p i (a t) -> p a i t", a=2),
+            )
+
+        for h in range(HKV):
+            weighted_values(h)
+            for u in range(2):
+                project_queries(h, u)
+                for bp in range(NB // 2):
+                    attend(h, u, bp)
+
+        out_v = out.rearrange("(k p) t -> p k t", p=P)
+        for o in range(ET):
+            o_ps = acc_psum.tile([P, L], F32, name="o_ps", tag="acc")
+            col = (o % 4) * P
+            for f in range(ET):
+                nc.tensor.matmul(
+                    o_ps[:], lhsT=wo_sb[o // 4][:, f, col : col + P], rhs=ctx_sb[f // 4][(f % 4) // 2][:, f % 2, :],
+                    start=(f == 0), stop=(f == ET - 1),
+                )
+            res = hid[o // 2][:, o % 2, :]
+            nc.vector.tensor_tensor(res, o_ps[:], res, ALU.add)
+            nc.sync.dma_start(out_v[:, o, :], res)

@@ -28,50 +28,50 @@ SCALE = 1.0 / math.sqrt(P)
 
 FLOPS = 2 * (2 * E * E * L) + 2 * (2 * ET * L * RUN * P)
 
+N_PAIR = ET // 2
+F_HALF = ET // 2
+
 
 def tile_hierarchicalsparseattention_b_kernel(tc, hidden, pre_norm_w, wq, wo, k_sel, v, wt, offs, out):
     nc = tc.nc
     with ExitStack() as ctx:
         held = ctx.enter_context(tc.tile_pool(name="held", bufs=1))
-        norm_ring = ctx.enter_context(tc.tile_pool(name="norm_ring", bufs=2))
-        work = ctx.enter_context(tc.tile_pool(name="work", bufs=3))
-        acc_psum = ctx.enter_context(tc.psum_pool(name="acc_psum", bufs=4))
+        work = ctx.enter_context(tc.tile_pool(name="work", bufs=2))
+        stats = ctx.enter_context(tc.tile_pool(name="stats", bufs=4))
+        acc_psum = ctx.enter_context(tc.psum_pool(name="acc_psum", bufs=3))
         s_psum = ctx.enter_context(tc.psum_pool(name="s_psum", bufs=2))
-        tp_psum = ctx.enter_context(tc.psum_pool(name="tp_psum", bufs=1))
+        tp_psum = ctx.enter_context(tc.psum_pool(name="tp_psum", bufs=2))
         ctx_psum = ctx.enter_context(tc.psum_pool(name="ctx_psum", bufs=1))
 
-        offsets = held.tile([P, N // 16], U16, name="offsets")
-        nc.sync.dma_start(offsets[:], offs)
-
-        w_rows = held.tile([P, P], F32, name="w_rows")
-        nc.vector.memset(w_rows[:], 0.0)
-        nc.sync.dma_start(w_rows[0:ET, :], pre_norm_w.rearrange("(k p) one -> k (p one)", p=P))
-
         hidden_v = hidden.rearrange("(k p) t -> p k t", p=P)
-        hid = [held.tile([P, 2, L], F32, name=f"hid{c}") for c in range(ET // 2)]
-        for c in range(ET // 2):
-            nc.sync.dma_start(hid[c][:], hidden_v[:, 2 * c : 2 * c + 2, :])
-
         wq_v = wq.rearrange("(k p) o -> p k o", p=P)
         wo_v = wo.rearrange("(k p) o -> p k o", p=P)
-        wq_sb = [held.tile([P, ET, GRP], BF16, name=f"wq{g}") for g in range(HKV)]
-        wo_sb = [held.tile([P, ET, GRP], BF16, name=f"wo{g}") for g in range(HKV)]
+        hid = [held.tile([P, 4, L], F32, name=f"hid{c}") for c in range(ET // 4)]
+        wq_sb = [held.tile([P, ET, 2 * P], BF16, name=f"wq{r}") for r in range(N_PAIR)]
+        wo_sb = [held.tile([P, ET, GRP], BF16, name=f"wo{g}") for g in range(ET // 4)]
         k_sb = [held.tile([P, N], BF16, name=f"k{h}") for h in range(HKV)]
         v_sb = [held.tile([P, S], F32, name=f"v{h}") for h in range(HKV)]
         wt_sb = [held.tile([P, N], F32, name=f"wt{h}") for h in range(HKV)]
+        offsets = held.tile([P, N // 16], U16, name="offsets")
+        w_rows = held.tile([P, P], F32, name="w_rows")
 
-        def load_weights(tile, view, g):
-            for half in range(2):
-                rows = slice(half * ET // 2, (half + 1) * ET // 2)
-                nc.sync.dma_start(tile[:, rows, :], view[:, rows, g * GRP : (g + 1) * GRP])
-
+        for c in range(ET // 4):
+            queue = nc.sync if c % 2 == 0 else nc.scalar
+            queue.dma_start(hid[c][:], hidden_v[:, 4 * c : 4 * c + 4, :])
+        nc.sync.dma_start(wq_sb[0][:], wq_v[:, :, 0 : 2 * P])
+        nc.scalar.dma_start(wq_sb[1][:], wq_v[:, :, 2 * P : 4 * P])
+        nc.vector.memset(w_rows[:], 0.0)
+        nc.sync.dma_start(w_rows[0:ET, :], pre_norm_w.rearrange("(k p) one -> k (p one)", p=P))
+        nc.sync.dma_start(offsets[:], offs)
         for h in range(HKV):
-            load_weights(wq_sb[h], wq_v, h)
             nc.sync.dma_start(k_sb[h][:], k_sel[h * P : (h + 1) * P, :])
             nc.sync.dma_start(v_sb[h][:], v[h * P : (h + 1) * P, :])
             nc.sync.dma_start(wt_sb[h][:], wt[h * P : (h + 1) * P, :])
-        for g in range(HKV):
-            load_weights(wo_sb[g], wo_v, g)
+            for r in range(2 * h + 2, min(2 * h + 4, N_PAIR)):
+                nc.sync.dma_start(wq_sb[r][:], wq_v[:, :, r * 2 * P : (r + 1) * 2 * P])
+        for rows in (slice(0, F_HALF), slice(F_HALF, ET)):
+            for g in range(ET // 4):
+                nc.sync.dma_start(wo_sb[g][:, rows, :], wo_v[:, rows, g * GRP : (g + 1) * GRP])
 
         ident_f = held.tile([P, P], F32, name="ident_f")
         make_identity(nc, ident_f[:])
@@ -82,30 +82,33 @@ def tile_hierarchicalsparseattention_b_kernel(tc, hidden, pre_norm_w, wq, wo, k_
         eps_col = held.tile([P, 1], F32, name="eps_col")
         nc.vector.memset(eps_col[:], EPS)
 
-        ss_ps = acc_psum.tile([P, L], F32, name="ss_ps", tag="acc")
-        for c in range(ET // 2):
-            sq = norm_ring.tile([P, 2, L], F32, name="sq")
-            nc.scalar.activation(sq[:], hid[c][:], FN.Square)
-            sq_sum = norm_ring.tile([P, L], F32, name="sq_sum")
-            nc.vector.tensor_tensor(sq_sum[:], sq[:, 0, :], sq[:, 1, :], ALU.add)
-            nc.tensor.matmul(ss_ps[:], lhsT=ones_f[:], rhs=sq_sum[:], start=(c == 0), stop=(c == ET // 2 - 1))
-        rstd = held.tile([P, L], F32, name="rstd")
-        nc.scalar.activation(rstd[:], ss_ps[:], FN.Abs_reciprocal_sqrt, bias=eps_col[:], scale=1.0 / E)
-
-        w_ps = tp_psum.tile([P, P], F32, name="w_ps", tag="tp")
-        nc.tensor.transpose(w_ps[:], w_rows[:], ident_f[:])
-        w_col = held.tile([P, ET], F32, name="w_col")
-        nc.vector.tensor_copy(w_col[:], w_ps[:, 0:ET])
-
         xn = [held.tile([P, L], BF16, name=f"xn{e}") for e in range(ET)]
-        for e in range(ET):
-            nc.vector.scalar_tensor_tensor(
-                xn[e][:], hid[e // 2][:, e % 2, :], w_col[:, e : e + 1], rstd[:], op0=ALU.mult, op1=ALU.mult
-            )
-
         vw_t = [held.tile([P, N // P, P], BF16, name=f"vw_t{h}") for h in range(HKV)]
-        q_sb = [[held.tile([P, NB, 2, BLK], BF16, name=f"q{h}_{u}") for u in range(2)] for h in range(HKV)]
-        ctx_sb = [[held.tile([P, 2, L], BF16, name=f"ctx{h}_{u}") for u in range(2)] for h in range(HKV)]
+        q_sb = [held.tile([P, NB, 2, BLK], BF16, name=f"q{r}") for r in range(N_PAIR)]
+        ctx_sb = [held.tile([P, 2, L], BF16, name=f"ctx{r}") for r in range(N_PAIR)]
+        prob_of = {}
+        prob_t_of = {}
+
+        def rms_norm():
+            ss_ps = acc_psum.tile([P, L], F32, name="ss_ps", tag="acc")
+            for c in range(ET // 2):
+                sq = work.tile([P, 2, L], F32, name="sq")
+                nc.scalar.activation(sq[:], hid[c // 2][:, 2 * (c % 2) : 2 * (c % 2) + 2, :], FN.Square)
+                sq_sum = work.tile([P, L], F32, name="sq_sum")
+                nc.vector.tensor_tensor(sq_sum[:], sq[:, 0, :], sq[:, 1, :], ALU.add)
+                nc.tensor.matmul(ss_ps[:], lhsT=ones_f[:], rhs=sq_sum[:], start=(c == 0), stop=(c == ET // 2 - 1))
+            rstd = held.tile([P, L], F32, name="rstd")
+            nc.scalar.activation(rstd[:], ss_ps[:], FN.Abs_reciprocal_sqrt, bias=eps_col[:], scale=1.0 / E)
+
+            w_ps = tp_psum.tile([P, P], F32, name="w_ps", tag="tp")
+            nc.tensor.transpose(w_ps[:], w_rows[:], ident_f[:])
+            w_col = held.tile([P, ET], F32, name="w_col")
+            nc.vector.tensor_copy(w_col[:], w_ps[:, 0:ET])
+
+            for e in range(ET):
+                nc.vector.scalar_tensor_tensor(
+                    xn[e][:], hid[e // 4][:, e % 4, :], w_col[:, e : e + 1], rstd[:], op0=ALU.mult, op1=ALU.mult
+                )
 
         def weighted_values(h):
             for piece in range(N // PIECE):
@@ -122,86 +125,107 @@ def tile_hierarchicalsparseattention_b_kernel(tc, hidden, pre_norm_w, wq, wo, k_
                 first = piece * PIECE // P
                 nc.scalar.copy(vw_t[h][:, first : first + PIECE // P, :], vw_ps[:])
 
-        def project_queries(h, u):
+        def project_queries(r):
             q_ps = [acc_psum.tile([P, L], F32, name=f"q_ps{a}", tag="acc") for a in range(2)]
             for e in range(ET):
                 for a in range(2):
-                    col = (2 * u + a) * P
                     nc.tensor.matmul(
-                        q_ps[a][:], lhsT=wq_sb[h][:, e, col : col + P], rhs=xn[e][:], start=(e == 0), stop=(e == ET - 1)
+                        q_ps[a][:], lhsT=wq_sb[r][:, e, a * P : (a + 1) * P], rhs=xn[e][:],
+                        start=(e == 0), stop=(e == ET - 1),
                     )
             for a in range(2):
-                nc.scalar.copy(q_sb[h][u][:, :, a, :], q_ps[a][:].rearrange("p (b t) -> p b t", b=NB))
+                nc.scalar.copy(q_sb[r][:, :, a, :], q_ps[a][:].rearrange("p (b t) -> p b t", b=NB))
 
-        def attend(h, u, bp):
-            s_ps = s_psum.tile([P, 2, RUN], F32, name="s_ps")
-            for i in range(2):
-                b = 2 * bp + i
-                nc.tensor.matmul(
-                    s_ps[:, i, :],
-                    lhsT=q_sb[h][u][:, b, :, :].rearrange("p a t -> p (a t)"),
-                    rhs=k_sb[h][:, b * RUN : (b + 1) * RUN],
-                    start=True,
-                    stop=True,
-                )
-            chunks = s_ps[:].rearrange("p i (k c) -> p (i k) c", c=BLK)
+        def scores(r):
             n_chunks = 2 * RUN // BLK
-            top = work.tile([P, n_chunks], F32, name="top")
-            nc.vector.reduce_max(top[:], chunks, axis=AXIS_X)
-            neg_m = work.tile([P, n_chunks], F32, name="neg_m")
-            nc.vector.tensor_scalar(neg_m[:], top[:], -SCALE, 0.0, op0=ALU.mult, op1=ALU.min)
-            ex = work.tile([P, n_chunks, BLK], F32, name="ex")
-            ex_sum = work.tile([P, n_chunks], F32, name="ex_sum")
-            for c in range(n_chunks):
-                nc.scalar.activation(
-                    ex[:, c, :], chunks[:, c, :], FN.Exp, bias=neg_m[:, c : c + 1], scale=SCALE,
-                    accum_out=ex_sum[:, c : c + 1],
+            chunks, neg_m, ex, ex_sum, one_term = [], [], [], [], []
+            for bp in range(NB // 2):
+                s_ps = s_psum.tile([P, 2, RUN], F32, name="s_ps")
+                for i in range(2):
+                    b = 2 * bp + i
+                    nc.tensor.matmul(
+                        s_ps[:, i, :],
+                        lhsT=q_sb[r][:, b, :, :].rearrange("p a t -> p (a t)"),
+                        rhs=k_sb[r // 2][:, b * RUN : (b + 1) * RUN],
+                        start=True,
+                        stop=True,
+                    )
+                chunks.append(s_ps[:].rearrange("p i (k c) -> p (i k) c", c=BLK))
+            for bp in range(NB // 2):
+                top = stats.tile([P, n_chunks], F32, name="top")
+                nc.vector.reduce_max(top[:], chunks[bp], axis=AXIS_X)
+                neg_m.append(stats.tile([P, n_chunks], F32, name="neg_m"))
+                nc.vector.tensor_scalar(neg_m[bp][:], top[:], -SCALE, 0.0, op0=ALU.mult, op1=ALU.min)
+            for bp in range(NB // 2):
+                ex.append(work.tile([P, n_chunks, BLK], F32, name="ex"))
+                ex_sum.append(stats.tile([P, n_chunks], F32, name="ex_sum"))
+                for c in range(n_chunks):
+                    nc.scalar.activation(
+                        ex[bp][:, c, :], chunks[bp][:, c, :], FN.Exp, bias=neg_m[bp][:, c : c + 1], scale=SCALE,
+                        accum_out=ex_sum[bp][:, c : c + 1],
+                    )
+                one_term.append(stats.tile([P, n_chunks], F32, name="one_term"))
+                nc.scalar.activation(one_term[bp][:], neg_m[bp][:], FN.Exp)
+            prob = work.tile([P, NB // 2, n_chunks, BLK], BF16, name="prob")
+            for bp in range(NB // 2):
+                den = stats.tile([P, n_chunks], F32, name="den")
+                nc.vector.tensor_tensor(den[:], ex_sum[bp][:], one_term[bp][:], ALU.add)
+                rden = stats.tile([P, n_chunks], F32, name="rden")
+                nc.vector.reciprocal(rden[:], den[:])
+                nc.vector.tensor_tensor(
+                    prob[:, bp, :, :], ex[bp][:], rden[:].unsqueeze(2).to_broadcast([P, n_chunks, BLK]), ALU.mult
                 )
-            one_term = work.tile([P, n_chunks], F32, name="one_term")
-            nc.scalar.activation(one_term[:], neg_m[:], FN.Exp)
-            den = work.tile([P, n_chunks], F32, name="den")
-            nc.vector.tensor_tensor(den[:], ex_sum[:], one_term[:], ALU.add)
-            rden = work.tile([P, n_chunks], F32, name="rden")
-            nc.vector.reciprocal(rden[:], den[:])
-            prob = work.tile([P, n_chunks, BLK], BF16, name="prob")
-            nc.vector.tensor_tensor(
-                prob[:], ex[:], rden[:].unsqueeze(2).to_broadcast([P, n_chunks, BLK]), ALU.mult
-            )
-            prob_cols = prob[:].rearrange("p k c -> p (k c)")
-            pt_ps = tp_psum.tile([P, 4, P], BF16, name="pt_ps", tag="tp")
-            for jt in range(4):
+            prob_of[r] = prob
+
+        def turn(r):
+            prob_cols = prob_of[r][:].rearrange("p b k c -> p (b k c)")
+            pt_ps = tp_psum.tile([P, N // P, P], BF16, name="pt_ps", tag="tp")
+            for jt in range(N // P):
                 nc.tensor.transpose(pt_ps[:, jt, :], prob_cols[:, jt * P : (jt + 1) * P], ident_b[:])
-            prob_t = work.tile([P, 4, P], BF16, name="prob_t")
+            prob_t = work.tile([P, N // P, P], BF16, name="prob_t")
             nc.scalar.copy(prob_t[:], pt_ps[:])
-            c_ps = ctx_psum.tile([P, 2, 2 * BLK], F32, name="c_ps")
-            for i in range(2):
-                b = 2 * bp + i
+            prob_t_of[r] = prob_t
+
+        def apply(r):
+            c_ps = ctx_psum.tile([P, NB, 2 * BLK], F32, name="c_ps")
+            for b in range(NB):
                 for jt in range(2):
                     nc.tensor.matmul(
-                        c_ps[:, i, :], lhsT=vw_t[h][:, 2 * b + jt, :], rhs=prob_t[:, 2 * i + jt, :],
+                        c_ps[:, b, :], lhsT=vw_t[r // 2][:, 2 * b + jt, :], rhs=prob_t_of[r][:, 2 * b + jt, :],
                         start=(jt == 0), stop=(jt == 1),
                     )
             nc.vector.tensor_copy(
-                ctx_sb[h][u][:, :, bp * 2 * BLK : (bp + 1) * 2 * BLK].rearrange("p a (i t) -> p a i t", i=2),
-                c_ps[:].rearrange("p i (a t) -> p a i t", a=2),
+                ctx_sb[r][:].rearrange("p a (b t) -> p a b t", b=NB), c_ps[:].rearrange("p b (a t) -> p a b t", a=2)
             )
 
-        for h in range(HKV):
-            weighted_values(h)
-            for u in range(2):
-                project_queries(h, u)
-                for bp in range(NB // 2):
-                    attend(h, u, bp)
-
         out_v = out.rearrange("(k p) t -> p k t", p=P)
-        for o in range(ET):
+
+        def project_output(o, f_first, f_last):
             o_ps = acc_psum.tile([P, L], F32, name="o_ps", tag="acc")
             col = (o % 4) * P
-            for f in range(ET):
+            for f in range(f_first, f_last + 1):
                 nc.tensor.matmul(
-                    o_ps[:], lhsT=wo_sb[o // 4][:, f, col : col + P], rhs=ctx_sb[f // 4][(f % 4) // 2][:, f % 2, :],
-                    start=(f == 0), stop=(f == ET - 1),
+                    o_ps[:], lhsT=wo_sb[o // 4][:, f, col : col + P], rhs=ctx_sb[f // 2][:, f % 2, :],
+                    start=(f == f_first), stop=(f == f_last),
                 )
-            res = hid[o // 2][:, o % 2, :]
+            res = hid[o // 4][:, o % 4, :]
             nc.vector.tensor_tensor(res, o_ps[:], res, ALU.add)
-            nc.sync.dma_start(out_v[:, o, :], res)
+
+        rms_norm()
+        for i in range(N_PAIR + ET // 4):
+            if i < N_PAIR:
+                project_queries(i)
+            else:
+                for o in range(4 * (i - N_PAIR), 4 * (i - N_PAIR) + 4):
+                    project_output(o, 0, F_HALF - 1)
+            if 0 <= i - 1 < N_PAIR:
+                scores(i - 1)
+            if 0 <= i - 3 < N_PAIR:
+                apply(i - 3)
+            if 0 <= i - 2 < N_PAIR:
+                turn(i - 2)
+            if i % 2 == 1 and i // 2 < HKV:
+                weighted_values(i // 2)
+        for o in range(ET):
+            project_output(o, F_HALF, ET - 1)
+            nc.sync.dma_start(out_v[:, o, :], hid[o // 4][:, o % 4, :])

@@ -47,30 +47,32 @@ def tile_hierarchicalsparseattention_b_kernel(tc, hidden, pre_norm_w, wq, wo, k_
         wq_v = wq.rearrange("(k p) o -> p k o", p=P)
         wo_v = wo.rearrange("(k p) o -> p k o", p=P)
         hid = [held.tile([P, 4, L], F32, name=f"hid{c}") for c in range(ET // 4)]
-        wq_sb = [held.tile([P, ET, 2 * P], BF16, name=f"wq{r}") for r in range(N_PAIR)]
+        wq_sb = [held.tile([P, ET, GRP], BF16, name=f"wq{g}") for g in range(HKV)]
         wo_sb = [held.tile([P, ET, GRP], BF16, name=f"wo{g}") for g in range(ET // 4)]
         k_sb = [held.tile([P, N], BF16, name=f"k{h}") for h in range(HKV)]
         v_sb = [held.tile([P, S], F32, name=f"v{h}") for h in range(HKV)]
         wt_sb = [held.tile([P, N], F32, name=f"wt{h}") for h in range(HKV)]
         offsets = held.tile([P, N // 16], U16, name="offsets")
         w_rows = held.tile([P, P], F32, name="w_rows")
+        halves = (slice(0, ET // 2), slice(ET // 2, ET))
 
+        nc.vector.memset(w_rows[:], 0.0)
+        nc.gpsimd.dma_start(w_rows[0:ET, :], pre_norm_w.rearrange("(k p) one -> k (p one)", p=P))
         for c in range(ET // 4):
             queue = nc.sync if c % 2 == 0 else nc.scalar
             queue.dma_start(hid[c][:], hidden_v[:, 4 * c : 4 * c + 4, :])
-        nc.sync.dma_start(wq_sb[0][:], wq_v[:, :, 0 : 2 * P])
-        nc.scalar.dma_start(wq_sb[1][:], wq_v[:, :, 2 * P : 4 * P])
-        nc.vector.memset(w_rows[:], 0.0)
-        nc.sync.dma_start(w_rows[0:ET, :], pre_norm_w.rearrange("(k p) one -> k (p one)", p=P))
+        nc.sync.dma_start(wq_sb[0][:, halves[0], :], wq_v[:, halves[0], 0:GRP])
+        nc.scalar.dma_start(wq_sb[0][:, halves[1], :], wq_v[:, halves[1], 0:GRP])
         nc.sync.dma_start(offsets[:], offs)
         for h in range(HKV):
             nc.sync.dma_start(k_sb[h][:], k_sel[h * P : (h + 1) * P, :])
             nc.sync.dma_start(v_sb[h][:], v[h * P : (h + 1) * P, :])
             nc.sync.dma_start(wt_sb[h][:], wt[h * P : (h + 1) * P, :])
-            for r in range(2 * h + 2, min(2 * h + 4, N_PAIR)):
-                nc.sync.dma_start(wq_sb[r][:], wq_v[:, :, r * 2 * P : (r + 1) * 2 * P])
-        for rows in (slice(0, F_HALF), slice(F_HALF, ET)):
-            for g in range(ET // 4):
+            if h + 1 < HKV:
+                for rows in halves:
+                    nc.sync.dma_start(wq_sb[h + 1][:, rows, :], wq_v[:, rows, (h + 1) * GRP : (h + 2) * GRP])
+        for g in range(ET // 4):
+            for rows in halves:
                 nc.sync.dma_start(wo_sb[g][:, rows, :], wo_v[:, rows, g * GRP : (g + 1) * GRP])
 
         ident_f = held.tile([P, P], F32, name="ident_f")
@@ -129,8 +131,9 @@ def tile_hierarchicalsparseattention_b_kernel(tc, hidden, pre_norm_w, wq, wo, k_
             q_ps = [acc_psum.tile([P, L], F32, name=f"q_ps{a}", tag="acc") for a in range(2)]
             for e in range(ET):
                 for a in range(2):
+                    col = (2 * (r % 2) + a) * P
                     nc.tensor.matmul(
-                        q_ps[a][:], lhsT=wq_sb[r][:, e, a * P : (a + 1) * P], rhs=xn[e][:],
+                        q_ps[a][:], lhsT=wq_sb[r // 2][:, e, col : col + P], rhs=xn[e][:],
                         start=(e == 0), stop=(e == ET - 1),
                     )
             for a in range(2):

@@ -43,37 +43,38 @@ def tile_hierarchicalsparseattention_b_kernel(tc, hidden, pre_norm_w, wq, wo, k_
         tp_psum = ctx.enter_context(tc.psum_pool(name="tp_psum", bufs=2))
         ctx_psum = ctx.enter_context(tc.psum_pool(name="ctx_psum", bufs=1))
 
+        offsets = held.tile([P, N // 16], U16, name="offsets")
+        nc.sync.dma_start(offsets[:], offs)
+
+        w_rows = held.tile([P, P], F32, name="w_rows")
+        nc.vector.memset(w_rows[:], 0.0)
+        nc.sync.dma_start(w_rows[0:ET, :], pre_norm_w.rearrange("(k p) one -> k (p one)", p=P))
+
         hidden_v = hidden.rearrange("(k p) t -> p k t", p=P)
+        hid = [held.tile([P, 2, L], F32, name=f"hid{c}") for c in range(ET // 2)]
+        for c in range(ET // 2):
+            nc.sync.dma_start(hid[c][:], hidden_v[:, 2 * c : 2 * c + 2, :])
+
         wq_v = wq.rearrange("(k p) o -> p k o", p=P)
         wo_v = wo.rearrange("(k p) o -> p k o", p=P)
-        hid = [held.tile([P, 4, L], F32, name=f"hid{c}") for c in range(ET // 4)]
         wq_sb = [held.tile([P, ET, GRP], BF16, name=f"wq{g}") for g in range(HKV)]
-        wo_sb = [held.tile([P, ET, GRP], BF16, name=f"wo{g}") for g in range(ET // 4)]
+        wo_sb = [held.tile([P, ET, GRP], BF16, name=f"wo{g}") for g in range(HKV)]
         k_sb = [held.tile([P, N], BF16, name=f"k{h}") for h in range(HKV)]
         v_sb = [held.tile([P, S], F32, name=f"v{h}") for h in range(HKV)]
         wt_sb = [held.tile([P, N], F32, name=f"wt{h}") for h in range(HKV)]
-        offsets = held.tile([P, N // 16], U16, name="offsets")
-        w_rows = held.tile([P, P], F32, name="w_rows")
-        halves = (slice(0, ET // 2), slice(ET // 2, ET))
 
-        nc.vector.memset(w_rows[:], 0.0)
-        nc.gpsimd.dma_start(w_rows[0:ET, :], pre_norm_w.rearrange("(k p) one -> k (p one)", p=P))
-        for c in range(ET // 4):
-            queue = nc.sync if c % 2 == 0 else nc.scalar
-            queue.dma_start(hid[c][:], hidden_v[:, 4 * c : 4 * c + 4, :])
-        nc.sync.dma_start(wq_sb[0][:, halves[0], :], wq_v[:, halves[0], 0:GRP])
-        nc.scalar.dma_start(wq_sb[0][:, halves[1], :], wq_v[:, halves[1], 0:GRP])
-        nc.sync.dma_start(offsets[:], offs)
+        def load_weights(tile, view, g):
+            for half in range(2):
+                rows = slice(half * ET // 2, (half + 1) * ET // 2)
+                nc.sync.dma_start(tile[:, rows, :], view[:, rows, g * GRP : (g + 1) * GRP])
+
         for h in range(HKV):
+            load_weights(wq_sb[h], wq_v, h)
             nc.sync.dma_start(k_sb[h][:], k_sel[h * P : (h + 1) * P, :])
             nc.sync.dma_start(v_sb[h][:], v[h * P : (h + 1) * P, :])
             nc.sync.dma_start(wt_sb[h][:], wt[h * P : (h + 1) * P, :])
-            if h + 1 < HKV:
-                for rows in halves:
-                    nc.sync.dma_start(wq_sb[h + 1][:, rows, :], wq_v[:, rows, (h + 1) * GRP : (h + 2) * GRP])
-        for g in range(ET // 4):
-            for rows in halves:
-                nc.sync.dma_start(wo_sb[g][:, rows, :], wo_v[:, rows, g * GRP : (g + 1) * GRP])
+        for g in range(HKV):
+            load_weights(wo_sb[g], wo_v, g)
 
         ident_f = held.tile([P, P], F32, name="ident_f")
         make_identity(nc, ident_f[:])
@@ -95,7 +96,7 @@ def tile_hierarchicalsparseattention_b_kernel(tc, hidden, pre_norm_w, wq, wo, k_
             ss_ps = acc_psum.tile([P, L], F32, name="ss_ps", tag="acc")
             for c in range(ET // 2):
                 sq = work.tile([P, 2, L], F32, name="sq")
-                nc.scalar.activation(sq[:], hid[c // 2][:, 2 * (c % 2) : 2 * (c % 2) + 2, :], FN.Square)
+                nc.scalar.activation(sq[:], hid[c][:], FN.Square)
                 sq_sum = work.tile([P, L], F32, name="sq_sum")
                 nc.vector.tensor_tensor(sq_sum[:], sq[:, 0, :], sq[:, 1, :], ALU.add)
                 nc.tensor.matmul(ss_ps[:], lhsT=ones_f[:], rhs=sq_sum[:], start=(c == 0), stop=(c == ET // 2 - 1))
@@ -109,7 +110,7 @@ def tile_hierarchicalsparseattention_b_kernel(tc, hidden, pre_norm_w, wq, wo, k_
 
             for e in range(ET):
                 nc.vector.scalar_tensor_tensor(
-                    xn[e][:], hid[e // 4][:, e % 4, :], w_col[:, e : e + 1], rstd[:], op0=ALU.mult, op1=ALU.mult
+                    xn[e][:], hid[e // 2][:, e % 2, :], w_col[:, e : e + 1], rstd[:], op0=ALU.mult, op1=ALU.mult
                 )
 
         def weighted_values(h):
@@ -211,7 +212,7 @@ def tile_hierarchicalsparseattention_b_kernel(tc, hidden, pre_norm_w, wq, wo, k_
                     o_ps[:], lhsT=wo_sb[o // 4][:, f, col : col + P], rhs=ctx_sb[f // 2][:, f % 2, :],
                     start=(f == f_first), stop=(f == f_last),
                 )
-            res = hid[o // 4][:, o % 4, :]
+            res = hid[o // 2][:, o % 2, :]
             nc.vector.tensor_tensor(res, o_ps[:], res, ALU.add)
 
         rms_norm()
@@ -231,4 +232,4 @@ def tile_hierarchicalsparseattention_b_kernel(tc, hidden, pre_norm_w, wq, wo, k_
                 weighted_values(i // 2)
         for o in range(ET):
             project_output(o, F_HALF, ET - 1)
-            nc.sync.dma_start(out_v[:, o, :], hid[o // 4][:, o % 4, :])
+            nc.sync.dma_start(out_v[:, o, :], hid[o // 2][:, o % 2, :])

@@ -122,9 +122,11 @@ def tile_hierarchicalsparseattention_b_kernel(tc, hidden, pre_norm_w, wq, wo, k_
                     wt_sb[h][:, piece * PIECE : (piece + 1) * PIECE],
                     ALU.mult,
                 )
-                vw_ps = tp_psum.tile([P, PIECE // P, P], F32, name="vw_ps", tag="tp")
+                vw_b = work.tile([P, PIECE], BF16, name="vw_b")
+                nc.gpsimd.tensor_copy(vw_b[:], vw[:])
+                vw_ps = tp_psum.tile([P, PIECE // P, P], BF16, name="vw_ps", tag="tp")
                 for jt in range(PIECE // P):
-                    nc.tensor.transpose(vw_ps[:, jt, :], vw[:, jt * P : (jt + 1) * P], ident_f[:])
+                    nc.tensor.transpose(vw_ps[:, jt, :], vw_b[:, jt * P : (jt + 1) * P], ident_b[:])
                 first = piece * PIECE // P
                 nc.scalar.copy(vw_t[h][:, first : first + PIECE // P, :], vw_ps[:])
 

@@ -89,6 +89,7 @@ def tile_hierarchicalsparseattention_b_kernel(tc, hidden, pre_norm_w, wq, wo, k_
         vw_t = [held.tile([P, N // P, P], BF16, name=f"vw_t{h}") for h in range(HKV)]
         q_sb = [held.tile([P, NB, 2, BLK], BF16, name=f"q{r}") for r in range(N_PAIR)]
         ctx_sb = [held.tile([P, 2, L], BF16, name=f"ctx{r}") for r in range(N_PAIR)]
+        vw_of = {}
         prob_of = {}
         prob_t_of = {}
 
@@ -114,21 +115,24 @@ def tile_hierarchicalsparseattention_b_kernel(tc, hidden, pre_norm_w, wq, wo, k_
                 )
 
         def weighted_values(h):
+            vw_b = work.tile([P, N], BF16, name="vw_b")
             for piece in range(N // PIECE):
+                cols = slice(piece * PIECE, (piece + 1) * PIECE)
                 vw = work.tile([P, PIECE], F32, name="vw")
                 nc.vector.tensor_tensor(
                     vw[:],
                     v_sb[h][:].indirect(offsets[:, piece * PIECE // 16 : (piece + 1) * PIECE // 16]),
-                    wt_sb[h][:, piece * PIECE : (piece + 1) * PIECE],
+                    wt_sb[h][:, cols],
                     ALU.mult,
                 )
-                vw_b = work.tile([P, PIECE], BF16, name="vw_b")
-                nc.gpsimd.tensor_copy(vw_b[:], vw[:])
-                vw_ps = tp_psum.tile([P, PIECE // P, P], BF16, name="vw_ps", tag="tp")
-                for jt in range(PIECE // P):
-                    nc.tensor.transpose(vw_ps[:, jt, :], vw_b[:, jt * P : (jt + 1) * P], ident_b[:])
-                first = piece * PIECE // P
-                nc.scalar.copy(vw_t[h][:, first : first + PIECE // P, :], vw_ps[:])
+                nc.gpsimd.tensor_copy(vw_b[:, cols], vw[:])
+            vw_of[h] = vw_b
+
+        def turn_values(h):
+            vw_ps = tp_psum.tile([P, N // P, P], BF16, name="vw_ps", tag="tp")
+            for jt in range(N // P):
+                nc.tensor.transpose(vw_ps[:, jt, :], vw_of[h][:, jt * P : (jt + 1) * P], ident_b[:])
+            nc.scalar.copy(vw_t[h][:], vw_ps[:])
 
         def project_queries(r):
             q_ps = [acc_psum.tile([P, L], F32, name=f"q_ps{a}", tag="acc") for a in range(2)]
@@ -230,6 +234,8 @@ def tile_hierarchicalsparseattention_b_kernel(tc, hidden, pre_norm_w, wq, wo, k_
                 apply(i - 3)
             if 0 <= i - 2 < N_PAIR:
                 turn(i - 2)
+            if i % 2 == 0 and 0 <= i // 2 - 1 < HKV:
+                turn_values(i // 2 - 1)
             if i % 2 == 1 and i // 2 < HKV:
                 weighted_values(i // 2)
         for o in range(ET):

@@ -29,6 +29,7 @@ SCALE = 1.0 / math.sqrt(P)
 FLOPS = 2 * (2 * E * E * L) + 2 * (2 * ET * L * RUN * P)
 
 N_PAIR = ET // 2
+STEPS = 16
 F_HALF = ET // 2
 
 
@@ -37,6 +38,7 @@ def tile_hierarchicalsparseattention_b_kernel(tc, hidden, pre_norm_w, wq, wo, k_
     with ExitStack() as ctx:
         held = ctx.enter_context(tc.tile_pool(name="held", bufs=1))
         work = ctx.enter_context(tc.tile_pool(name="work", bufs=2))
+        prob_pool = ctx.enter_context(tc.tile_pool(name="prob_pool", bufs=3))
         stats = ctx.enter_context(tc.tile_pool(name="stats", bufs=4))
         acc_psum = ctx.enter_context(tc.psum_pool(name="acc_psum", bufs=3))
         s_psum = ctx.enter_context(tc.psum_pool(name="s_psum", bufs=2))
@@ -92,11 +94,15 @@ def tile_hierarchicalsparseattention_b_kernel(tc, hidden, pre_norm_w, wq, wo, k_
         vw_of = {}
         prob_of = {}
         prob_t_of = {}
+        q_ps_of = {}
+        o_ps_of = {}
+        pt_ps_of = {}
+        vw_ps_of = {}
 
         def rms_norm():
             ss_ps = acc_psum.tile([P, L], F32, name="ss_ps", tag="acc")
             for c in range(ET // 2):
-                sq = work.tile([P, 2, L], F32, name="sq")
+                sq = work.tile([P, 2, L], F32, name="sq", tag="ex")
                 nc.scalar.activation(sq[:], hid[c][:], FN.Square)
                 sq_sum = work.tile([P, L], F32, name="sq_sum")
                 nc.vector.tensor_tensor(sq_sum[:], sq[:, 0, :], sq[:, 1, :], ALU.add)
@@ -128,23 +134,25 @@ def tile_hierarchicalsparseattention_b_kernel(tc, hidden, pre_norm_w, wq, wo, k_
                 nc.gpsimd.tensor_copy(vw_b[:, cols], vw[:])
             vw_of[h] = vw_b
 
-        def turn_values(h):
-            vw_ps = tp_psum.tile([P, N // P, P], BF16, name="vw_ps", tag="tp")
-            for jt in range(N // P):
-                nc.tensor.transpose(vw_ps[:, jt, :], vw_of[h][:, jt * P : (jt + 1) * P], ident_b[:])
-            nc.scalar.copy(vw_t[h][:], vw_ps[:])
+        def turn_values(h, jt):
+            if jt == 0:
+                vw_ps_of[h] = tp_psum.tile([P, N // P, P], BF16, name="vw_ps", tag="tp")
+            nc.tensor.transpose(vw_ps_of[h][:, jt, :], vw_of[h][:, jt * P : (jt + 1) * P], ident_b[:])
+            if jt == N // P - 1:
+                nc.scalar.copy(vw_t[h][:], vw_ps_of[h][:])
 
-        def project_queries(r):
-            q_ps = [acc_psum.tile([P, L], F32, name=f"q_ps{a}", tag="acc") for a in range(2)]
-            for e in range(ET):
-                for a in range(2):
-                    col = (2 * (r % 2) + a) * P
-                    nc.tensor.matmul(
-                        q_ps[a][:], lhsT=wq_sb[r // 2][:, e, col : col + P], rhs=xn[e][:],
-                        start=(e == 0), stop=(e == ET - 1),
-                    )
+        def project_queries(r, e):
+            if e == 0:
+                q_ps_of[r] = [acc_psum.tile([P, L], F32, name=f"q_ps{a}", tag="acc") for a in range(2)]
             for a in range(2):
-                nc.scalar.copy(q_sb[r][:, :, a, :], q_ps[a][:].rearrange("p (b t) -> p b t", b=NB))
+                col = (2 * (r % 2) + a) * P
+                nc.tensor.matmul(
+                    q_ps_of[r][a][:], lhsT=wq_sb[r // 2][:, e, col : col + P], rhs=xn[e][:],
+                    start=(e == 0), stop=(e == ET - 1),
+                )
+            if e == ET - 1:
+                for a in range(2):
+                    nc.scalar.copy(q_sb[r][:, :, a, :], q_ps_of[r][a][:].rearrange("p (b t) -> p b t", b=NB))
 
         def scores(r):
             n_chunks = 2 * RUN // BLK
@@ -176,7 +184,7 @@ def tile_hierarchicalsparseattention_b_kernel(tc, hidden, pre_norm_w, wq, wo, k_
                     )
                 one_term.append(stats.tile([P, n_chunks], F32, name="one_term"))
                 nc.scalar.activation(one_term[bp][:], neg_m[bp][:], FN.Exp)
-            prob = work.tile([P, NB // 2, n_chunks, BLK], BF16, name="prob")
+            prob = prob_pool.tile([P, NB // 2, n_chunks, BLK], BF16, name="prob")
             for bp in range(NB // 2):
                 den = stats.tile([P, n_chunks], F32, name="den")
                 nc.vector.tensor_tensor(den[:], ex_sum[bp][:], one_term[bp][:], ALU.add)
@@ -187,14 +195,15 @@ def tile_hierarchicalsparseattention_b_kernel(tc, hidden, pre_norm_w, wq, wo, k_
                 )
             prob_of[r] = prob
 
-        def turn(r):
+        def turn(r, jt):
+            if jt == 0:
+                pt_ps_of[r] = tp_psum.tile([P, N // P, P], BF16, name="pt_ps", tag="tp")
             prob_cols = prob_of[r][:].rearrange("p b k c -> p (b k c)")
-            pt_ps = tp_psum.tile([P, N // P, P], BF16, name="pt_ps", tag="tp")
-            for jt in range(N // P):
-                nc.tensor.transpose(pt_ps[:, jt, :], prob_cols[:, jt * P : (jt + 1) * P], ident_b[:])
-            prob_t = work.tile([P, N // P, P], BF16, name="prob_t")
-            nc.scalar.copy(prob_t[:], pt_ps[:])
-            prob_t_of[r] = prob_t
+            nc.tensor.transpose(pt_ps_of[r][:, jt, :], prob_cols[:, jt * P : (jt + 1) * P], ident_b[:])
+            if jt == N // P - 1:
+                prob_t = work.tile([P, N // P, P], BF16, name="prob_t")
+                nc.scalar.copy(prob_t[:], pt_ps_of[r][:])
+                prob_t_of[r] = prob_t
 
         def apply(r):
             c_ps = ctx_psum.tile([P, NB, 2 * BLK], F32, name="c_ps")
@@ -210,34 +219,37 @@ def tile_hierarchicalsparseattention_b_kernel(tc, hidden, pre_norm_w, wq, wo, k_
 
         out_v = out.rearrange("(k p) t -> p k t", p=P)
 
-        def project_output(o, f_first, f_last):
-            o_ps = acc_psum.tile([P, L], F32, name="o_ps", tag="acc")
+        def project_output(o, f, f_first, f_last):
+            if f == f_first:
+                o_ps_of[o] = acc_psum.tile([P, L], F32, name="o_ps", tag="acc")
             col = (o % 4) * P
-            for f in range(f_first, f_last + 1):
-                nc.tensor.matmul(
-                    o_ps[:], lhsT=wo_sb[o // 4][:, f, col : col + P], rhs=ctx_sb[f // 2][:, f % 2, :],
-                    start=(f == f_first), stop=(f == f_last),
-                )
-            res = hid[o // 2][:, o % 2, :]
-            nc.vector.tensor_tensor(res, o_ps[:], res, ALU.add)
+            nc.tensor.matmul(
+                o_ps_of[o][:], lhsT=wo_sb[o // 4][:, f, col : col + P], rhs=ctx_sb[f // 2][:, f % 2, :],
+                start=(f == f_first), stop=(f == f_last),
+            )
+            if f == f_last:
+                res = hid[o // 2][:, o % 2, :]
+                nc.vector.tensor_tensor(res, o_ps_of[o][:], res, ALU.add)
 
         rms_norm()
         for i in range(N_PAIR + ET // 4):
-            if i < N_PAIR:
-                project_queries(i)
-            else:
-                for o in range(4 * (i - N_PAIR), 4 * (i - N_PAIR) + 4):
-                    project_output(o, 0, F_HALF - 1)
+            for s in range(STEPS):
+                if i < N_PAIR:
+                    project_queries(i, s)
+                else:
+                    for f in (2 * (s % 4), 2 * (s % 4) + 1):
+                        project_output(4 * (i - N_PAIR) + s // 4, f, 0, F_HALF - 1)
+                if s % 2 == 0 and 0 <= i - 3 < N_PAIR:
+                    turn(i - 3, s // 2)
+                if s % 2 == 1 and i % 2 == 0 and 0 <= i // 2 - 1 < HKV:
+                    turn_values(i // 2 - 1, s // 2)
             if 0 <= i - 1 < N_PAIR:
                 scores(i - 1)
-            if 0 <= i - 3 < N_PAIR:
-                apply(i - 3)
-            if 0 <= i - 2 < N_PAIR:
-                turn(i - 2)
-            if i % 2 == 0 and 0 <= i // 2 - 1 < HKV:
-                turn_values(i // 2 - 1)
+            if 0 <= i - 4 < N_PAIR:
+                apply(i - 4)
             if i % 2 == 1 and i // 2 < HKV:
                 weighted_values(i // 2)
         for o in range(ET):
-            project_output(o, F_HALF, ET - 1)
+            for f in range(F_HALF, ET):
+                project_output(o, f, F_HALF, ET - 1)
             nc.sync.dma_start(out_v[:, o, :], hid[o // 2][:, o % 2, :])

@@ -40,10 +40,9 @@ def tile_hierarchicalsparseattention_b_kernel(tc, hidden, pre_norm_w, wq, wo, k_
         work = ctx.enter_context(tc.tile_pool(name="work", bufs=2))
         prob_pool = ctx.enter_context(tc.tile_pool(name="prob_pool", bufs=3))
         stats = ctx.enter_context(tc.tile_pool(name="stats", bufs=4))
-        acc_psum = ctx.enter_context(tc.psum_pool(name="acc_psum", bufs=3))
+        acc_psum = ctx.enter_context(tc.psum_pool(name="acc_psum", bufs=4))
         s_psum = ctx.enter_context(tc.psum_pool(name="s_psum", bufs=2))
         tp_psum = ctx.enter_context(tc.psum_pool(name="tp_psum", bufs=2))
-        ctx_psum = ctx.enter_context(tc.psum_pool(name="ctx_psum", bufs=1))
 
         offsets = held.tile([P, N // 16], U16, name="offsets")
         nc.sync.dma_start(offsets[:], offs)
@@ -141,18 +140,16 @@ def tile_hierarchicalsparseattention_b_kernel(tc, hidden, pre_norm_w, wq, wo, k_
             if jt == N // P - 1:
                 nc.scalar.copy(vw_t[h][:], vw_ps_of[h][:])
 
-        def project_queries(r, e):
+        def project_queries(r, a, e):
             if e == 0:
-                q_ps_of[r] = [acc_psum.tile([P, L], F32, name=f"q_ps{a}", tag="acc") for a in range(2)]
-            for a in range(2):
-                col = (2 * (r % 2) + a) * P
-                nc.tensor.matmul(
-                    q_ps_of[r][a][:], lhsT=wq_sb[r // 2][:, e, col : col + P], rhs=xn[e][:],
-                    start=(e == 0), stop=(e == ET - 1),
-                )
+                q_ps_of[r, a] = acc_psum.tile([P, L], F32, name="q_ps", tag="acc")
+            col = (2 * (r % 2) + a) * P
+            nc.tensor.matmul(
+                q_ps_of[r, a][:], lhsT=wq_sb[r // 2][:, e, col : col + P], rhs=xn[e][:],
+                start=(e == 0), stop=(e == ET - 1),
+            )
             if e == ET - 1:
-                for a in range(2):
-                    nc.scalar.copy(q_sb[r][:, :, a, :], q_ps_of[r][a][:].rearrange("p (b t) -> p b t", b=NB))
+                nc.scalar.copy(q_sb[r][:, :, a, :], q_ps_of[r, a][:].rearrange("p (b t) -> p b t", b=NB))
 
         def scores(r):
             n_chunks = 2 * RUN // BLK
@@ -206,7 +203,7 @@ def tile_hierarchicalsparseattention_b_kernel(tc, hidden, pre_norm_w, wq, wo, k_
                 prob_t_of[r] = prob_t
 
         def apply(r):
-            c_ps = ctx_psum.tile([P, NB, 2 * BLK], F32, name="c_ps")
+            c_ps = acc_psum.tile([P, NB, 2 * BLK], F32, name="c_ps", tag="acc")
             for b in range(NB):
                 for jt in range(2):
                     nc.tensor.matmul(
@@ -232,10 +229,14 @@ def tile_hierarchicalsparseattention_b_kernel(tc, hidden, pre_norm_w, wq, wo, k_
                 nc.vector.tensor_tensor(res, o_ps_of[o][:], res, ALU.add)
 
         rms_norm()
-        for i in range(N_PAIR + ET // 4):
+        for i in range(1, N_PAIR + ET // 4):
             for s in range(STEPS):
-                if i < N_PAIR:
-                    project_queries(i, s)
+                if i == 1:
+                    for head in range(4):
+                        project_queries(head // 2, head % 2, s)
+                elif i < N_PAIR:
+                    for e in (2 * (s % 8), 2 * (s % 8) + 1):
+                        project_queries(i, s // 8, e)
                 else:
                     for f in (2 * (s % 4), 2 * (s % 4) + 1):
                         project_output(4 * (i - N_PAIR) + s // 4, f, 0, F_HALF - 1)

@@ -49,7 +49,7 @@ def tile_hierarchicalsparseattention_b_kernel(tc, hidden, pre_norm_w, wq, wo, k_
 
         w_rows = held.tile([P, P], F32, name="w_rows")
         nc.vector.memset(w_rows[:], 0.0)
-        nc.sync.dma_start(w_rows[0:ET, :], pre_norm_w.rearrange("(k p) one -> k (p one)", p=P))
+        nc.scalar.dma_start(w_rows[0:ET, :], pre_norm_w.rearrange("(k p) one -> k (p one)", p=P))
 
         hidden_v = hidden.rearrange("(k p) t -> p k t", p=P)
         hid = [held.tile([P, 2, L], F32, name=f"hid{c}") for c in range(ET // 2)]
@@ -100,12 +100,16 @@ def tile_hierarchicalsparseattention_b_kernel(tc, hidden, pre_norm_w, wq, wo, k_
 
         def rms_norm():
             ss_ps = acc_psum.tile([P, L], F32, name="ss_ps", tag="acc")
+            sq_sum = {}
             for c in range(ET // 2):
                 sq = work.tile([P, 2, L], F32, name="sq", tag="ex")
                 nc.scalar.activation(sq[:], hid[c][:], FN.Square)
-                sq_sum = work.tile([P, L], F32, name="sq_sum")
-                nc.vector.tensor_tensor(sq_sum[:], sq[:, 0, :], sq[:, 1, :], ALU.add)
-                nc.tensor.matmul(ss_ps[:], lhsT=ones_f[:], rhs=sq_sum[:], start=(c == 0), stop=(c == ET // 2 - 1))
+                sq_sum[c] = work.tile([P, L], F32, name="sq_sum")
+                nc.vector.tensor_tensor(sq_sum[c][:], sq[:, 0, :], sq[:, 1, :], ALU.add)
+                if c % 2 == 1:
+                    sq_four = work.tile([P, L], F32, name="sq_four")
+                    nc.vector.tensor_tensor(sq_four[:], sq_sum[c - 1][:], sq_sum[c][:], ALU.add)
+                    nc.tensor.matmul(ss_ps[:], lhsT=ones_f[:], rhs=sq_four[:], start=(c == 1), stop=(c == ET // 2 - 1))
             rstd = held.tile([P, L], F32, name="rstd")
             nc.scalar.activation(rstd[:], ss_ps[:], FN.Abs_reciprocal_sqrt, bias=eps_col[:], scale=1.0 / E)
 

@@ -39,6 +39,7 @@ def tile_hierarchicalsparseattention_b_kernel(tc, hidden, pre_norm_w, wq, wo, k_
         held = ctx.enter_context(tc.tile_pool(name="held", bufs=1))
         work = ctx.enter_context(tc.tile_pool(name="work", bufs=2))
         prob_pool = ctx.enter_context(tc.tile_pool(name="prob_pool", bufs=3))
+        vw_pool = ctx.enter_context(tc.tile_pool(name="vw_pool", bufs=1))
         stats = ctx.enter_context(tc.tile_pool(name="stats", bufs=4))
         acc_psum = ctx.enter_context(tc.psum_pool(name="acc_psum", bufs=4))
         s_psum = ctx.enter_context(tc.psum_pool(name="s_psum", bufs=2))
@@ -124,7 +125,7 @@ def tile_hierarchicalsparseattention_b_kernel(tc, hidden, pre_norm_w, wq, wo, k_
                 )
 
         def weighted_values(h):
-            vw_b = work.tile([P, N], BF16, name="vw_b")
+            vw_b = vw_pool.tile([P, N], BF16, name="vw_b")
             for piece in range(N // PIECE):
                 cols = slice(piece * PIECE, (piece + 1) * PIECE)
                 vw = work.tile([P, PIECE], F32, name="vw")

@@ -41,8 +41,8 @@ def tile_hierarchicalsparseattention_b_kernel(tc, hidden, pre_norm_w, wq, wo, k_
         prob_pool = ctx.enter_context(tc.tile_pool(name="prob_pool", bufs=3))
         vw_pool = ctx.enter_context(tc.tile_pool(name="vw_pool", bufs=1))
         stats = ctx.enter_context(tc.tile_pool(name="stats", bufs=4))
-        acc_psum = ctx.enter_context(tc.psum_pool(name="acc_psum", bufs=4))
-        s_psum = ctx.enter_context(tc.psum_pool(name="s_psum", bufs=2))
+        acc_psum = ctx.enter_context(tc.psum_pool(name="acc_psum", bufs=3))
+        s_psum = ctx.enter_context(tc.psum_pool(name="s_psum", bufs=3))
         tp_psum = ctx.enter_context(tc.psum_pool(name="tp_psum", bufs=2))
 
         offsets = held.tile([P, N // 16], U16, name="offsets")
@@ -50,12 +50,13 @@ def tile_hierarchicalsparseattention_b_kernel(tc, hidden, pre_norm_w, wq, wo, k_
 
         w_rows = held.tile([P, P], F32, name="w_rows")
         nc.vector.memset(w_rows[:], 0.0)
-        nc.scalar.dma_start(w_rows[0:ET, :], pre_norm_w.rearrange("(k p) one -> k (p one)", p=P))
 
         hidden_v = hidden.rearrange("(k p) t -> p k t", p=P)
         hid = [held.tile([P, 2, L], F32, name=f"hid{c}") for c in range(ET // 2)]
         for c in range(ET // 2):
             nc.sync.dma_start(hid[c][:], hidden_v[:, 2 * c : 2 * c + 2, :])
+            if c == 0:
+                nc.sync.dma_start(w_rows[0:ET, :], pre_norm_w.rearrange("(k p) one -> k (p one)", p=P))
 
         wq_v = wq.rearrange("(k p) o -> p k o", p=P)
         wo_v = wo.rearrange("(k p) o -> p k o", p=P)
@@ -146,15 +147,15 @@ def tile_hierarchicalsparseattention_b_kernel(tc, hidden, pre_norm_w, wq, wo, k_
                 nc.scalar.copy(vw_t[h][:], vw_ps_of[h][:])
 
         def project_queries(r, a, e):
-            if e == 0:
-                q_ps_of[r, a] = acc_psum.tile([P, L], F32, name="q_ps", tag="acc")
+            if a == 0 and e == 0:
+                q_ps_of[r] = acc_psum.tile([P, 2, L], F32, name="q_ps", tag="acc")
             col = (2 * (r % 2) + a) * P
             nc.tensor.matmul(
-                q_ps_of[r, a][:], lhsT=wq_sb[r // 2][:, e, col : col + P], rhs=xn[e][:],
+                q_ps_of[r][:, a, :], lhsT=wq_sb[r // 2][:, e, col : col + P], rhs=xn[e][:],
                 start=(e == 0), stop=(e == ET - 1),
             )
-            if e == ET - 1:
-                nc.scalar.copy(q_sb[r][:, :, a, :], q_ps_of[r, a][:].rearrange("p (b t) -> p b t", b=NB))
+            if a == 1 and e == ET - 1:
+                nc.scalar.copy(q_sb[r][:], q_ps_of[r][:].rearrange("p a (b t) -> p b a t", b=NB))
 
         def scores(r):
             n_chunks = 2 * RUN // BLK
@@ -237,8 +238,9 @@ def tile_hierarchicalsparseattention_b_kernel(tc, hidden, pre_norm_w, wq, wo, k_
         for i in range(1, N_PAIR + ET // 4):
             for s in range(STEPS):
                 if i == 1:
-                    for head in range(4):
-                        project_queries(head // 2, head % 2, s)
+                    for e in (2 * (s % 8), 2 * (s % 8) + 1):
+                        for r in range(2):
+                            project_queries(r, s // 8, e)
                 elif i < N_PAIR:
                     for e in (2 * (s % 8), 2 * (s % 8) + 1):
                         project_queries(i, s // 8, e)

@@ -193,7 +193,7 @@ def tile_hierarchicalsparseattention_b_kernel(tc, hidden, pre_norm_w, wq, wo, k_
                 nc.vector.tensor_tensor(den[:], ex_sum[bp][:], one_term[bp][:], ALU.add)
                 rden = stats.tile([P, n_chunks], F32, name="rden")
                 nc.vector.reciprocal(rden[:], den[:])
-                nc.vector.tensor_tensor(
+                (nc.gpsimd if bp == 1 else nc.vector).tensor_tensor(
                     prob[:, bp, :, :], ex[bp][:], rden[:].unsqueeze(2).to_broadcast([P, n_chunks, BLK]), ALU.mult
                 )
             prob_of[r] = prob

@@ -101,17 +101,25 @@ def tile_hierarchicalsparseattention_b_kernel(tc, hidden, pre_norm_w, wq, wo, k_
         vw_ps_of = {}
 
         def rms_norm():
+            last = ET // 2 - 1
             ss_ps = acc_psum.tile([P, L], F32, name="ss_ps", tag="acc")
             sq_sum = {}
             for c in range(ET // 2):
-                sq = work.tile([P, 2, L], F32, name="sq", tag="ex")
-                nc.scalar.activation(sq[:], hid[c][:], FN.Square)
-                sq_sum[c] = work.tile([P, L], F32, name="sq_sum")
+                sq = (work if c % 2 == 0 else prob_pool).tile([P, 2, L], F32, name="sq", tag="ex" if c % 2 == 0 else "prob")
+                if c % 2 == 0:
+                    nc.scalar.activation(sq[:], hid[c][:], FN.Square)
+                else:
+                    helper = nc.vector if c == last else nc.gpsimd
+                    nc.scalar.activation(sq[:, 0, :], hid[c][:, 0, :], FN.Square)
+                    helper.tensor_tensor(sq[:, 1, :], hid[c][:, 1, :], hid[c][:, 1, :], ALU.mult)
+                sq_sum[c] = work.tile([P, L], F32, name="sq_sum", tag="sq_sum" if c % 2 == 0 else "vw")
                 nc.vector.tensor_tensor(sq_sum[c][:], sq[:, 0, :], sq[:, 1, :], ALU.add)
-                if c % 2 == 1:
+                if c >= 4:
+                    nc.tensor.matmul(ss_ps[:], lhsT=ones_f[:], rhs=sq_sum[c][:], start=False, stop=(c == last))
+                elif c % 2 == 1:
                     sq_four = work.tile([P, L], F32, name="sq_four")
                     nc.vector.tensor_tensor(sq_four[:], sq_sum[c - 1][:], sq_sum[c][:], ALU.add)
-                    nc.tensor.matmul(ss_ps[:], lhsT=ones_f[:], rhs=sq_four[:], start=(c == 1), stop=(c == ET // 2 - 1))
+                    nc.tensor.matmul(ss_ps[:], lhsT=ones_f[:], rhs=sq_four[:], start=(c == 1), stop=False)
             rstd = held.tile([P, L], F32, name="rstd")
             nc.scalar.activation(rstd[:], ss_ps[:], FN.Abs_reciprocal_sqrt, bias=eps_col[:], scale=1.0 / E)
 
@@ -159,7 +167,9 @@ def tile_hierarchicalsparseattention_b_kernel(tc, hidden, pre_norm_w, wq, wo, k_
 
         def scores(r):
             n_chunks = 2 * RUN // BLK
-            chunks, neg_m, ex, ex_sum, one_term = [], [], [], [], []
+            chunks, ex, ex_sum = [], [], []
+            neg_m = stats.tile([P, NB // 2, n_chunks], F32, name="neg_m")
+            one_term = stats.tile([P, NB // 2, n_chunks], F32, name="one_term")
             for bp in range(NB // 2):
                 s_ps = s_psum.tile([P, 2, RUN], F32, name="s_ps")
                 for i in range(2):
@@ -175,22 +185,21 @@ def tile_hierarchicalsparseattention_b_kernel(tc, hidden, pre_norm_w, wq, wo, k_
             for bp in range(NB // 2):
                 top = stats.tile([P, n_chunks], F32, name="top")
                 nc.vector.reduce_max(top[:], chunks[bp], axis=AXIS_X)
-                neg_m.append(stats.tile([P, n_chunks], F32, name="neg_m"))
-                nc.vector.tensor_scalar(neg_m[bp][:], top[:], -SCALE, 0.0, op0=ALU.mult, op1=ALU.min)
+                nc.vector.tensor_scalar(neg_m[:, bp, :], top[:], -SCALE, 0.0, op0=ALU.mult, op1=ALU.min)
             for bp in range(NB // 2):
                 ex.append(work.tile([P, n_chunks, BLK], F32, name="ex"))
                 ex_sum.append(stats.tile([P, n_chunks], F32, name="ex_sum"))
                 for c in range(n_chunks):
                     nc.scalar.activation(
-                        ex[bp][:, c, :], chunks[bp][:, c, :], FN.Exp, bias=neg_m[bp][:, c : c + 1], scale=SCALE,
+                        ex[bp][:, c, :], chunks[bp][:, c, :], FN.Exp, bias=neg_m[:, bp, c : c + 1], scale=SCALE,
                         accum_out=ex_sum[bp][:, c : c + 1],
                     )
-                one_term.append(stats.tile([P, n_chunks], F32, name="one_term"))
-                nc.scalar.activation(one_term[bp][:], neg_m[bp][:], FN.Exp)
+                if bp == 0:
+                    nc.scalar.activation(one_term[:], neg_m[:], FN.Exp)
             prob = prob_pool.tile([P, NB // 2, n_chunks, BLK], BF16, name="prob")
             for bp in range(NB // 2):
                 den = stats.tile([P, n_chunks], F32, name="den")
-                nc.vector.tensor_tensor(den[:], ex_sum[bp][:], one_term[bp][:], ALU.add)
+                nc.vector.tensor_tensor(den[:], ex_sum[bp][:], one_term[:, bp, :], ALU.add)
                 rden = stats.tile([P, n_chunks], F32, name="rden")
                 nc.vector.reciprocal(rden[:], den[:])
                 (nc.gpsimd if bp == 1 else nc.vector).tensor_tensor(
@@ -222,16 +231,16 @@ def tile_hierarchicalsparseattention_b_kernel(tc, hidden, pre_norm_w, wq, wo, k_
 
         out_v = out.rearrange("(k p) t -> p k t", p=P)
 
-        def project_output(o, f, f_first, f_last):
+        def project_output(o, f, f_first, f_last, tokens=slice(0, L)):
             if f == f_first:
-                o_ps_of[o] = acc_psum.tile([P, L], F32, name="o_ps", tag="acc")
+                o_ps_of[o] = acc_psum.tile([P, tokens.stop - tokens.start], F32, name="o_ps", tag="acc")
             col = (o % 4) * P
             nc.tensor.matmul(
-                o_ps_of[o][:], lhsT=wo_sb[o // 4][:, f, col : col + P], rhs=ctx_sb[f // 2][:, f % 2, :],
+                o_ps_of[o][:], lhsT=wo_sb[o // 4][:, f, col : col + P], rhs=ctx_sb[f // 2][:, f % 2, tokens],
                 start=(f == f_first), stop=(f == f_last),
             )
             if f == f_last:
-                res = hid[o // 2][:, o % 2, :]
+                res = hid[o // 2][:, o % 2, tokens]
                 nc.vector.tensor_tensor(res, o_ps_of[o][:], res, ALU.add)
 
         rms_norm()
@@ -251,13 +260,14 @@ def tile_hierarchicalsparseattention_b_kernel(tc, hidden, pre_norm_w, wq, wo, k_
                     turn(i - 3, s // 2)
                 if s % 2 == 1 and i % 2 == 0 and 0 <= i // 2 - 1 < HKV:
                     turn_values(i // 2 - 1, s // 2)
-            if 0 <= i - 1 < N_PAIR:
-                scores(i - 1)
             if 0 <= i - 4 < N_PAIR:
                 apply(i - 4)
+            if 0 <= i - 1 < N_PAIR:
+                scores(i - 1)
             if i % 2 == 1 and i // 2 < HKV:
                 weighted_values(i // 2)
         for o in range(ET):
-            for f in range(F_HALF, ET):
-                project_output(o, f, F_HALF, ET - 1)
-            nc.sync.dma_start(out_v[:, o, :], hid[o // 2][:, o % 2, :])
+            for tokens in [slice(0, L)] if o < ET - 1 else [slice(0, L // 2), slice(L // 2, L)]:
+                for f in range(F_HALF, ET):
+                    project_output(o, f, F_HALF, ET - 1, tokens)
+                nc.sync.dma_start(out_v[:, o, tokens], hid[o // 2][:, o % 2, tokens])

import math
from contextlib import ExitStack

import concourse.mybir as mybir
from concourse.masks import make_identity

F32 = mybir.dt.float32
BF16 = mybir.dt.bfloat16
U16 = mybir.dt.uint16
ALU = mybir.AluOpType
FN = mybir.ActivationFunctionType
AXIS_X = mybir.AxisListType.X

P = 128
E = 2048
ET = E // P
L = 256
HKV = 4
BLK = 64
NB = 4
RUN = 256
S = 512
N = 1024
PIECE = 512
GRP = 512
EPS = 1e-6
SCALE = 1.0 / math.sqrt(P)

FLOPS = 2 * (2 * E * E * L) + 2 * (2 * ET * L * RUN * P)

N_PAIR = ET // 2
STEPS = 16
F_HALF = ET // 2


def tile_hierarchicalsparseattention_b_kernel(tc, hidden, pre_norm_w, wq, wo, k_sel, v, wt, offs, out):
    nc = tc.nc
    with ExitStack() as ctx:
        held = ctx.enter_context(tc.tile_pool(name="held", bufs=1))
        work = ctx.enter_context(tc.tile_pool(name="work", bufs=2))
        prob_pool = ctx.enter_context(tc.tile_pool(name="prob_pool", bufs=3))
        vw_pool = ctx.enter_context(tc.tile_pool(name="vw_pool", bufs=1))
        stats = ctx.enter_context(tc.tile_pool(name="stats", bufs=4))
        acc_psum = ctx.enter_context(tc.psum_pool(name="acc_psum", bufs=3))
        s_psum = ctx.enter_context(tc.psum_pool(name="s_psum", bufs=3))
        tp_psum = ctx.enter_context(tc.psum_pool(name="tp_psum", bufs=2))

        offsets = held.tile([P, N // 16], U16, name="offsets")
        nc.sync.dma_start(offsets[:], offs)

        w_rows = held.tile([P, P], F32, name="w_rows")
        nc.vector.memset(w_rows[:], 0.0)

        hidden_v = hidden.rearrange("(k p) t -> p k t", p=P)
        hid = [held.tile([P, 2, L], F32, name=f"hid{c}") for c in range(ET // 2)]
        for c in range(ET // 2):
            nc.sync.dma_start(hid[c][:], hidden_v[:, 2 * c : 2 * c + 2, :])
            if c == 0:
                nc.sync.dma_start(w_rows[0:ET, :], pre_norm_w.rearrange("(k p) one -> k (p one)", p=P))

        wq_v = wq.rearrange("(k p) o -> p k o", p=P)
        wo_v = wo.rearrange("(k p) o -> p k o", p=P)
        wq_sb = [held.tile([P, ET, GRP], BF16, name=f"wq{g}") for g in range(HKV)]
        wo_sb = [held.tile([P, ET, GRP], BF16, name=f"wo{g}") for g in range(HKV)]
        k_sb = [held.tile([P, N], BF16, name=f"k{h}") for h in range(HKV)]
        v_sb = [held.tile([P, S], F32, name=f"v{h}") for h in range(HKV)]
        wt_sb = [held.tile([P, N], F32, name=f"wt{h}") for h in range(HKV)]

        def load_weights(tile, view, g):
            for half in range(2):
                rows = slice(half * ET // 2, (half + 1) * ET // 2)
                nc.sync.dma_start(tile[:, rows, :], view[:, rows, g * GRP : (g + 1) * GRP])

        for h in range(HKV):
            load_weights(wq_sb[h], wq_v, h)
            nc.sync.dma_start(k_sb[h][:], k_sel[h * P : (h + 1) * P, :])
            nc.sync.dma_start(v_sb[h][:], v[h * P : (h + 1) * P, :])
            nc.sync.dma_start(wt_sb[h][:], wt[h * P : (h + 1) * P, :])
        for g in range(HKV):
            load_weights(wo_sb[g], wo_v, g)

        ident_f = held.tile([P, P], F32, name="ident_f")
        make_identity(nc, ident_f[:])
        ident_b = held.tile([P, P], BF16, name="ident_b")
        make_identity(nc, ident_b[:])
        ones_f = held.tile([P, P], F32, name="ones_f")
        nc.vector.memset(ones_f[:], 1.0)
        eps_col = held.tile([P, 1], F32, name="eps_col")
        nc.vector.memset(eps_col[:], EPS)

        xn = [held.tile([P, L], BF16, name=f"xn{e}") for e in range(ET)]
        vw_t = [held.tile([P, N // P, P], BF16, name=f"vw_t{h}") for h in range(HKV)]
        q_sb = [held.tile([P, NB, 2, BLK], BF16, name=f"q{r}") for r in range(N_PAIR)]
        ctx_sb = [held.tile([P, 2, L], BF16, name=f"ctx{r}") for r in range(N_PAIR)]
        vw_of = {}
        prob_of = {}
        prob_t_of = {}
        q_ps_of = {}
        o_ps_of = {}
        pt_ps_of = {}
        vw_ps_of = {}

        def rms_norm():
            last = ET // 2 - 1
            ss_ps = acc_psum.tile([P, L], F32, name="ss_ps", tag="acc")
            sq_sum = {}
            for c in range(ET // 2):
                sq = (work if c % 2 == 0 else prob_pool).tile([P, 2, L], F32, name="sq", tag="ex" if c % 2 == 0 else "prob")
                if c % 2 == 0:
                    nc.scalar.activation(sq[:], hid[c][:], FN.Square)
                else:
                    helper = nc.vector if c == last else nc.gpsimd
                    nc.scalar.activation(sq[:, 0, :], hid[c][:, 0, :], FN.Square)
                    helper.tensor_tensor(sq[:, 1, :], hid[c][:, 1, :], hid[c][:, 1, :], ALU.mult)
                sq_sum[c] = work.tile([P, L], F32, name="sq_sum", tag="sq_sum" if c % 2 == 0 else "vw")
                nc.vector.tensor_tensor(sq_sum[c][:], sq[:, 0, :], sq[:, 1, :], ALU.add)
                if c >= 4:
                    nc.tensor.matmul(ss_ps[:], lhsT=ones_f[:], rhs=sq_sum[c][:], start=False, stop=(c == last))
                elif c % 2 == 1:
                    sq_four = work.tile([P, L], F32, name="sq_four")
                    nc.vector.tensor_tensor(sq_four[:], sq_sum[c - 1][:], sq_sum[c][:], ALU.add)
                    nc.tensor.matmul(ss_ps[:], lhsT=ones_f[:], rhs=sq_four[:], start=(c == 1), stop=False)
            rstd = held.tile([P, L], F32, name="rstd")
            nc.scalar.activation(rstd[:], ss_ps[:], FN.Abs_reciprocal_sqrt, bias=eps_col[:], scale=1.0 / E)

            w_ps = tp_psum.tile([P, P], F32, name="w_ps", tag="tp")
            nc.tensor.transpose(w_ps[:], w_rows[:], ident_f[:])
            w_col = held.tile([P, ET], F32, name="w_col")
            nc.vector.tensor_copy(w_col[:], w_ps[:, 0:ET])

            for e in range(ET):
                nc.vector.scalar_tensor_tensor(
                    xn[e][:], hid[e // 2][:, e % 2, :], w_col[:, e : e + 1], rstd[:], op0=ALU.mult, op1=ALU.mult
                )

        def weighted_values(h):
            vw_b = vw_pool.tile([P, N], BF16, name="vw_b")
            for piece in range(N // PIECE):
                cols = slice(piece * PIECE, (piece + 1) * PIECE)
                vw = work.tile([P, PIECE], F32, name="vw")
                nc.vector.tensor_tensor(
                    vw[:],
                    v_sb[h][:].indirect(offsets[:, piece * PIECE // 16 : (piece + 1) * PIECE // 16]),
                    wt_sb[h][:, cols],
                    ALU.mult,
                )
                nc.gpsimd.tensor_copy(vw_b[:, cols], vw[:])
            vw_of[h] = vw_b

        def turn_values(h, jt):
            if jt == 0:
                vw_ps_of[h] = tp_psum.tile([P, N // P, P], BF16, name="vw_ps", tag="tp")
            nc.tensor.transpose(vw_ps_of[h][:, jt, :], vw_of[h][:, jt * P : (jt + 1) * P], ident_b[:])
            if jt == N // P - 1:
                nc.scalar.copy(vw_t[h][:], vw_ps_of[h][:])

        def project_queries(r, a, e):
            if a == 0 and e == 0:
                q_ps_of[r] = acc_psum.tile([P, 2, L], F32, name="q_ps", tag="acc")
            col = (2 * (r % 2) + a) * P
            nc.tensor.matmul(
                q_ps_of[r][:, a, :], lhsT=wq_sb[r // 2][:, e, col : col + P], rhs=xn[e][:],
                start=(e == 0), stop=(e == ET - 1),
            )
            if a == 1 and e == ET - 1:
                nc.scalar.copy(q_sb[r][:], q_ps_of[r][:].rearrange("p a (b t) -> p b a t", b=NB))

        def scores(r):
            n_chunks = 2 * RUN // BLK
            chunks, ex, ex_sum = [], [], []
            neg_m = stats.tile([P, NB // 2, n_chunks], F32, name="neg_m")
            one_term = stats.tile([P, NB // 2, n_chunks], F32, name="one_term")
            for bp in range(NB // 2):
                s_ps = s_psum.tile([P, 2, RUN], F32, name="s_ps")
                for i in range(2):
                    b = 2 * bp + i
                    nc.tensor.matmul(
                        s_ps[:, i, :],
                        lhsT=q_sb[r][:, b, :, :].rearrange("p a t -> p (a t)"),
                        rhs=k_sb[r // 2][:, b * RUN : (b + 1) * RUN],
                        start=True,
                        stop=True,
                    )
                chunks.append(s_ps[:].rearrange("p i (k c) -> p (i k) c", c=BLK))
            for bp in range(NB // 2):
                top = stats.tile([P, n_chunks], F32, name="top")
                nc.vector.reduce_max(top[:], chunks[bp], axis=AXIS_X)
                nc.vector.tensor_scalar(neg_m[:, bp, :], top[:], -SCALE, 0.0, op0=ALU.mult, op1=ALU.min)
            for bp in range(NB // 2):
                ex.append(work.tile([P, n_chunks, BLK], F32, name="ex"))
                ex_sum.append(stats.tile([P, n_chunks], F32, name="ex_sum"))
                for c in range(n_chunks):
                    nc.scalar.activation(
                        ex[bp][:, c, :], chunks[bp][:, c, :], FN.Exp, bias=neg_m[:, bp, c : c + 1], scale=SCALE,
                        accum_out=ex_sum[bp][:, c : c + 1],
                    )
                if bp == 0:
                    nc.scalar.activation(one_term[:], neg_m[:], FN.Exp)
            prob = prob_pool.tile([P, NB // 2, n_chunks, BLK], BF16, name="prob")
            for bp in range(NB // 2):
                den = stats.tile([P, n_chunks], F32, name="den")
                nc.vector.tensor_tensor(den[:], ex_sum[bp][:], one_term[:, bp, :], ALU.add)
                rden = stats.tile([P, n_chunks], F32, name="rden")
                nc.vector.reciprocal(rden[:], den[:])
                (nc.gpsimd if bp == 1 else nc.vector).tensor_tensor(
                    prob[:, bp, :, :], ex[bp][:], rden[:].unsqueeze(2).to_broadcast([P, n_chunks, BLK]), ALU.mult
                )
            prob_of[r] = prob

        def turn(r, jt):
            if jt == 0:
                pt_ps_of[r] = tp_psum.tile([P, N // P, P], BF16, name="pt_ps", tag="tp")
            prob_cols = prob_of[r][:].rearrange("p b k c -> p (b k c)")
            nc.tensor.transpose(pt_ps_of[r][:, jt, :], prob_cols[:, jt * P : (jt + 1) * P], ident_b[:])
            if jt == N // P - 1:
                prob_t = work.tile([P, N // P, P], BF16, name="prob_t")
                nc.scalar.copy(prob_t[:], pt_ps_of[r][:])
                prob_t_of[r] = prob_t

        def apply(r):
            c_ps = acc_psum.tile([P, NB, 2 * BLK], F32, name="c_ps", tag="acc")
            for b in range(NB):
                for jt in range(2):
                    nc.tensor.matmul(
                        c_ps[:, b, :], lhsT=vw_t[r // 2][:, 2 * b + jt, :], rhs=prob_t_of[r][:, 2 * b + jt, :],
                        start=(jt == 0), stop=(jt == 1),
                    )
            nc.vector.tensor_copy(
                ctx_sb[r][:].rearrange("p a (b t) -> p a b t", b=NB), c_ps[:].rearrange("p b (a t) -> p a b t", a=2)
            )

        out_v = out.rearrange("(k p) t -> p k t", p=P)

        def project_output(o, f, f_first, f_last, tokens=slice(0, L)):
            if f == f_first:
                o_ps_of[o] = acc_psum.tile([P, tokens.stop - tokens.start], F32, name="o_ps", tag="acc")
            col = (o % 4) * P
            nc.tensor.matmul(
                o_ps_of[o][:], lhsT=wo_sb[o // 4][:, f, col : col + P], rhs=ctx_sb[f // 2][:, f % 2, tokens],
                start=(f == f_first), stop=(f == f_last),
            )
            if f == f_last:
                res = hid[o // 2][:, o % 2, tokens]
                nc.vector.tensor_tensor(res, o_ps_of[o][:], res, ALU.add)

        rms_norm()
        for i in range(1, N_PAIR + ET // 4):
            for s in range(STEPS):
                if i == 1:
                    for e in (2 * (s % 8), 2 * (s % 8) + 1):
                        for r in range(2):
                            project_queries(r, s // 8, e)
                elif i < N_PAIR:
                    for e in (2 * (s % 8), 2 * (s % 8) + 1):
                        project_queries(i, s // 8, e)
                else:
                    for f in (2 * (s % 4), 2 * (s % 4) + 1):
                        project_output(4 * (i - N_PAIR) + s // 4, f, 0, F_HALF - 1)
                if s % 2 == 0 and 0 <= i - 3 < N_PAIR:
                    turn(i - 3, s // 2)
                if s % 2 == 1 and i % 2 == 0 and 0 <= i // 2 - 1 < HKV:
                    turn_values(i // 2 - 1, s // 2)
            if 0 <= i - 4 < N_PAIR:
                apply(i - 4)
            if 0 <= i - 1 < N_PAIR:
                scores(i - 1)
            if i % 2 == 1 and i // 2 < HKV:
                weighted_values(i // 2)
        for o in range(ET):
            for tokens in [slice(0, L)] if o < ET - 1 else [slice(0, L // 2), slice(L // 2, L)]:
                for f in range(F_HALF, ET):
                    project_output(o, f, F_HALF, ET - 1, tokens)
                nc.sync.dma_start(out_v[:, o, tokens], hid[o // 2][:, o % 2, tokens])
